import numpy as np
import ml_dtypes


def mxq(x, axis, fmt="e4m3"):
    dtype, down = {"e4m3": (ml_dtypes.float8_e4m3fn, 7), "e5m2": (ml_dtypes.float8_e5m2, 14)}[fmt]
    v = np.moveaxis(np.asarray(x, np.float32).astype(ml_dtypes.bfloat16).astype(np.float64), axis, -1)
    blocks = v.reshape(v.shape[:-1] + (-1, 32))
    amax = np.abs(blocks).max(-1, keepdims=True)
    byte = np.maximum(np.where(amax > 0, np.frexp(amax)[1] - 1 + 127, 0) - down, 1)
    scale = np.exp2(byte - 127.0)
    codes = (blocks / scale).astype(np.float32).astype(dtype).astype(np.float64)
    return np.moveaxis((codes * scale).reshape(v.shape), -1, axis)


WIDE = False


def mx_kscale(k):
    if not WIDE:
        return np.ones(k)
    levels = np.array([30, -30])
    if k % 512:
        return np.exp2(np.random.permutation(np.resize(levels, k // 32))).repeat(32)
    a = np.empty((k // 512, 16))
    for p in range(k // 512):
        a[p, :8] = np.random.permutation(np.resize(levels, 8))
        for g in range(8):
            far = levels[np.abs(levels - a[p, g]) >= 10]
            a[p, g + 8] = far[np.random.randint(len(far))]
    return np.exp2(a.ravel()).repeat(32)


BF16 = ml_dtypes.bfloat16


def bf(x):
    return np.asarray(x, np.float32).astype(BF16)


def f64(x):
    return np.asarray(x).astype(np.float64)


E2M1 = np.array([0.0, 0.5, 1.0, 1.5, 2.0, 3.0, 4.0, 6.0, -0.0, -0.5, -1.0, -1.5, -2.0, -3.0, -4.0, -6.0])


def pack_weight(w, fmt):
    k, n = w.shape
    w = f64(bf(w)).reshape(k // 32, 32, n)
    amax = np.abs(w).max(1)
    if fmt == "e4m3":
        byte = np.frexp(amax)[1] - 1 + 127 - 7
    else:
        mant, ex = np.frexp(amax / 6.0)
        byte = np.where(mant > 0.5, ex, ex - 1) + 127
    byte = np.clip(np.where(amax > 0, byte, 1), 1, 254)
    scaled = (w * np.exp2(127.0 - byte)[:, None, :]).reshape(k, n).astype(np.float32)
    by_word = np.ascontiguousarray(scaled.reshape(k // 512, 128, 4, n).transpose(0, 1, 3, 2))
    if fmt == "e4m3":
        words = by_word.astype(ml_dtypes.float8_e4m3fn).view(np.uint8)
    else:
        c = by_word.astype(ml_dtypes.float4_e2m1fn).view(np.uint8) & 0xF
        words = c[..., 0::2] | (c[..., 1::2] << 4)
    return np.ascontiguousarray(words), np.ascontiguousarray(byte.astype(np.uint8).reshape(k // 512, 16, n))


def unpack_weight(words, scales, fmt):
    g, p, n, _ = words.shape
    if fmt == "e4m3":
        vals = np.ascontiguousarray(words).view(ml_dtypes.float8_e4m3fn).astype(np.float64)
    else:
        nib = np.empty((g, p, n, 4), np.uint8)
        nib[..., 0::2] = words & 0xF
        nib[..., 1::2] = words >> 4
        vals = E2M1[nib]
    vals = vals * np.repeat(np.exp2(scales.astype(np.float64) - 127.0), 8, axis=1)[..., None]
    return vals.transpose(0, 1, 3, 2).reshape(g * 512, n)

def pack4(w):
    words, scales = pack_weight(w, "e2m1")
    return words.reshape(words.shape[0], 128, -1), scales


def unpack4(words, scales):
    return unpack_weight(words.reshape(words.shape[0], 128, -1, 2), scales, "e2m1")


B, S, D, H, DK = 4, 128, 2048, 16, 128
E = H * DK
HALF = DK // 2


def rope(t, cos2, sin2):
    t_even = t[..., 0::2]
    t_odd = t[..., 1::2]
    rot = np.stack([-t_odd, t_even], axis=-1).reshape(t.shape)
    return t * cos2 + rot * sin2


def setup_inputs():
    s = mx_kscale(D)
    ang = np.random.uniform(-np.pi, np.pi, (S, HALF))
    x = bf(np.random.standard_normal((B, S, D)) * s)
    Wq_words, Wq_scales = pack4(np.random.standard_normal((D, E)) / np.sqrt(D) / s[:, None])
    Wk_words, Wk_scales = pack4(np.random.standard_normal((D, E)) / np.sqrt(D) / s[:, None])
    return {"x": x,
            "Wq_words": Wq_words,
            "Wq_scales": Wq_scales,
            "Wk_words": Wk_words,
            "Wk_scales": Wk_scales,
            "cos2": bf(np.repeat(np.cos(ang), 2, axis=-1)),
            "sin2": bf(np.repeat(np.sin(ang), 2, axis=-1))}


def reference(x, Wq_words, Wq_scales, Wk_words, Wk_scales, cos2, sin2):
    xq = mxq(f64(x), 2, "e5m2")
    q = (xq @ unpack4(Wq_words, Wq_scales)).reshape(B, S, H, DK).swapaxes(1, 2)
    k = (xq @ unpack4(Wk_words, Wk_scales)).reshape(B, S, H, DK).swapaxes(1, 2)
    c, sn = f64(cos2), f64(sin2)
    return rope(q, c, sn), rope(k, c, sn)

@@ -1,0 +1,210 @@
+from contextlib import ExitStack
+
+import concourse.mybir as mybir
+from concourse.masks import make_identity
+
+B, S, D, H, DK = 4, 128, 2048, 16, 128
+E = H * DK
+FLOPS = 2 * (B * S) * D * (2 * E)
+
+F32 = mybir.dt.float32
+BF16 = mybir.dt.bfloat16
+U32 = mybir.dt.uint32
+U8 = mybir.dt.uint8
+I32 = mybir.dt.int32
+E5M2X4 = mybir.dt.float8_e5m2_x4
+E2M1X4 = mybir.dt.float4_e2m1fn_x4
+MULT = mybir.AluOpType.mult
+ADD = mybir.AluOpType.add
+COPY = mybir.ActivationFunctionType.Copy
+
+P = 128
+G = D // 512
+NB = 512
+HB = NB // DK
+NJ = E // NB
+
+MANUAL = True
+ACC_BUFS = 6
+WORK_BUFS = 3
+PREP_AFTER = 2
+FIRST_ADDS = (512, 512, 1024)
+MID_ADDS = (1024, 1024)
+LAST_ADDS = (1024, 512, 512)
+
+
+def tile_multiheadselfattention_pa_kernel(
+    tc, x, Wq_words, Wq_scales, Wk_words, Wk_scales, cos2, sin2, out_0, out_1
+):
+    nc = tc.nc
+    w_words = (Wq_words, Wk_words)
+    w_scales = (Wq_scales, Wk_scales)
+    outs = (out_0, out_1)
+
+    with ExitStack() as ctx:
+        keep = ctx.enter_context(tc.tile_pool(name="keep", bufs=1))
+        work = ctx.enter_context(tc.tile_pool(name="work", bufs=WORK_BUFS))
+        acc_pool = ctx.enter_context(tc.psum_pool(name="accp", bufs=ACC_BUFS))
+        xt_pool = ctx.enter_context(tc.psum_pool(name="xtp", bufs=2))
+        if MANUAL:
+            ctx.enter_context(tc.manual_schedule())
+
+        warm = keep.tile([P, 8], F32, name="warm")
+        warm2 = keep.tile([P, 8], F32, name="warm2")
+        nc.vector.memset(warm[:], 0.0)
+        nc.scalar.activation(out=warm2[:], in_=warm[:], func=COPY)
+
+        plane_of = {}
+        plane_list = []
+        for w, c0, ncols in ((0, 0, 1024), (0, 1024, 1024), (1, 0, 2048)):
+            plane = keep.tile([P, G, ncols], U8, name="plane%d_%d" % (w, c0), align_bytes=64)
+            nc.vector.memset(plane[:].rearrange("p g n -> p (g n)").bitcast(I32), 0)
+            plane_list.append((plane, w, c0, ncols))
+            for c in range(c0, c0 + ncols, NB):
+                plane_of[(w, c // NB)] = (plane, c - c0)
+
+        cos_bf = keep.tile([P, DK], BF16, name="cos_bf")
+        sin_bf = keep.tile([P, DK], BF16, name="sin_bf")
+        nc.gpsimd.dma_start(out=cos_bf[:], in_=cos2)
+        nc.gpsimd.dma_start(out=sin_bf[:], in_=sin2)
+        ident = keep.tile([P, P], F32, name="ident")
+        make_identity(nc, ident[:])
+
+        x_sb = []
+        for m in range(B):
+            xs = keep.tile([P, D], BF16, name="x%d" % m)
+            x_sb.append(xs)
+        nc.scalar.dma_start(out=x_sb[0][:, 0:1024], in_=x[0][:, 0:1024])
+        nc.scalar.dma_start(out=x_sb[0][:, 1024:2048], in_=x[0][:, 1024:2048])
+
+        w_sb = {}
+
+        def load_scales(i):
+            plane, w, c0, ncols = plane_list[i]
+            for q in range(4):
+                nc.sync.dma_start(
+                    out=plane[32 * q : 32 * q + 4, :, :].bitcast(I32),
+                    in_=w_scales[w][:, 4 * q : 4 * q + 4, c0 : c0 + ncols].rearrange("g r n -> r g n").bitcast(I32),
+                )
+
+        def load_words(w, c0, ncols):
+            wt = keep.tile([P, G, 2 * ncols], U8, name="w%d_%d" % (w, c0), align_bytes=64)
+            nc.sync.dma_start(
+                out=wt[:].bitcast(I32),
+                in_=w_words[w][:, :, 2 * c0 : 2 * (c0 + ncols)].rearrange("g p n -> p g n").bitcast(I32),
+            )
+            for c in range(c0, c0 + ncols, NB):
+                w_sb[(w, c // NB)] = (wt, c - c0)
+
+        load_words(0, 0, 512)
+        load_scales(0)
+        load_words(0, 512, 512)
+        nc.sync.dma_start(out=x_sb[1][:], in_=x[1])
+        load_scales(1)
+        load_words(0, 1024, 512)
+        load_words(0, 1536, 512)
+        nc.sync.dma_start(out=x_sb[2][:], in_=x[2])
+        nc.sync.dma_start(out=x_sb[3][:], in_=x[3])
+        load_scales(2)
+        load_words(1, 0, 1024)
+        load_words(1, 1024, 1024)
+
+        cos4 = keep.tile([P, HB, DK], F32, name="cos4")
+        sin4 = keep.tile([P, HB, DK], F32, name="sin4")
+        nc.gpsimd.tensor_scalar(
+            out=cos4[:],
+            in0=cos_bf[:].rearrange("p (o d) -> p o d", o=1).to_broadcast([P, HB, DK]),
+            scalar1=1.0,
+            scalar2=0.0,
+            op0=MULT,
+            op1=ADD,
+        )
+
+        def sin_tables():
+            for e, sign in ((0, -1.0), (1, 1.0)):
+                nc.scalar.activation(
+                    out=sin4[:, :, e:DK:2],
+                    in_=sin_bf[:, e:DK:2].rearrange("p (o d) -> p o d", o=1).to_broadcast([P, HB, DK // 2]),
+                    func=COPY,
+                    scale=sign,
+                )
+
+        x_codes = []
+        x_scl = []
+        for m in range(B):
+            xc = keep.tile([P, G, P], U32, name="xc%d" % m, align_bytes=64)
+            xl = keep.tile([P, G, P], U8, name="xl%d" % m, align_bytes=64)
+            x_codes.append(xc)
+            x_scl.append(xl)
+
+        def prep(m):
+            words = x_sb[m][:].bitcast(F32)
+            grouped = keep.tile([P, D], BF16, name="grp%d" % m, align_bytes=64)
+            gview = grouped[:].bitcast(F32).rearrange("p (g r u) -> p g r u", g=G, u=2)
+            for half in range(2):
+                xt = xt_pool.tile([P, 4, P], F32, name="xt")
+                for gg in range(2):
+                    g = 2 * half + gg
+                    for u in range(2):
+                        nc.tensor.transpose(xt[:, 2 * gg + u, :], words[:, 256 * g + u : 256 * (g + 1) : 2], ident[:])
+                nc.scalar.copy(
+                    out=gview[:, 2 * half : 2 * half + 2],
+                    in_=xt[:].rearrange("p (g u) r -> p g r u", u=2),
+                )
+                nc.vector.quantize_mx(
+                    out=x_codes[m][:, 2 * half : 2 * half + 2, :].rearrange("p g r -> p (g r)").bitcast(E5M2X4),
+                    scales=x_scl[m][:, 2 * half : 2 * half + 2, :].rearrange("p g r -> p (g r)"),
+                    in_=grouped[:, 1024 * half : 1024 * (half + 1)],
+                )
+
+        def bank(w, m, jj, ta, tb):
+            wt, off = w_sb[(w, jj)]
+            plane, poff = plane_of[(w, jj)]
+            acc = acc_pool.tile([P, NB], F32, name="acc")
+            for g in range(G):
+                nc.tensor.matmul_mx(
+                    out=acc[:],
+                    lhsT=x_codes[m][:, g, :].bitcast(E5M2X4),
+                    lhsT_scale=x_scl[m][:, g, :],
+                    rhs=wt[:, g, 2 * off : 2 * (off + NB)].bitcast(E2M1X4),
+                    rhs_scale=plane[:, g, poff : poff + NB],
+                    start=(g == 0),
+                    stop=(g == G - 1),
+                )
+            cols = slice(NB * jj, NB * (jj + 1))
+            nc.vector.tensor_tensor(out=ta[:, cols], in0=acc[:], in1=cos4[:].rearrange("p h d -> p (h d)"), op=MULT)
+            nc.vector.tensor_tensor(
+                out=tb[:, cols].rearrange("p (n e) -> p n e", e=2),
+                in0=acc[:].rearrange("p (n e) -> p n e", e=2)[:, :, ::-1],
+                in1=sin4[:].rearrange("p h (n e) -> p (h n) e", e=2),
+                op=MULT,
+            )
+
+        prep(0)
+        sin_tables()
+        for w in range(2):
+            for m in range(B):
+                ta = work.tile([P, E], F32, name="ta")
+                tb = work.tile([P, E], F32, name="tb")
+                to = work.tile([P, E], F32, name="to")
+                adds = MID_ADDS
+                if w == 0 and m == 0:
+                    adds = FIRST_ADDS
+                if w == 1 and m == B - 1:
+                    adds = LAST_ADDS
+                ends = []
+                c = 0
+                for width in adds:
+                    ends.append((c, c + width))
+                    c += width
+                for jj in range(NJ):
+                    if w == 0 and m + 1 < B and jj == PREP_AFTER:
+                        prep(m + 1)
+                    bank(w, m, jj, ta, tb)
+                    for c0, c1 in ends:
+                        if c1 == NB * (jj + 1):
+                            nc.gpsimd.tensor_tensor(out=to[:, c0:c1], in0=ta[:, c0:c1], in1=tb[:, c0:c1], op=ADD)
+                            nc.sync.dma_start(
+                                out=outs[w][m, c0 // DK : c1 // DK].rearrange("h s d -> s h d"),
+                                in_=to[:, c0:c1].rearrange("p (h d) -> p h d", d=DK),
+                            )

@@ -24,13 +24,17 @@ NB = 512
 HB = NB // DK
 NJ = E // NB
 
-MANUAL = True
-ACC_BUFS = 6
 WORK_BUFS = 3
 PREP_AFTER = 2
-FIRST_ADDS = (512, 512, 1024)
-MID_ADDS = (1024, 1024)
-LAST_ADDS = (1024, 512, 512)
+FIRST_ADDS = ((512, 0), (512, 0), (1024, 0))
+MID_ADDS = ((1024, 0), (1024, 0))
+LAST_ADDS = ((512, 0), (512, 1), (512, 1), (512, 1))
+PERMUTE = True
+WARM = 4
+X0_PIECES = ((0, 1), (2,), (3,))
+XM_PIECES = ((0, 1), (2, 3))
+SCALES_BY_R = False
+STORE_ALT = False
 
 
 def tile_multiheadselfattention_pa_kernel(
@@ -44,48 +48,64 @@ def tile_multiheadselfattention_pa_kernel(
     with ExitStack() as ctx:
         keep = ctx.enter_context(tc.tile_pool(name="keep", bufs=1))
         work = ctx.enter_context(tc.tile_pool(name="work", bufs=WORK_BUFS))
-        acc_pool = ctx.enter_context(tc.psum_pool(name="accp", bufs=ACC_BUFS))
-        xt_pool = ctx.enter_context(tc.psum_pool(name="xtp", bufs=2))
-        if MANUAL:
-            ctx.enter_context(tc.manual_schedule())
-
-        warm = keep.tile([P, 8], F32, name="warm")
-        warm2 = keep.tile([P, 8], F32, name="warm2")
-        nc.vector.memset(warm[:], 0.0)
-        nc.scalar.activation(out=warm2[:], in_=warm[:], func=COPY)
-
-        plane_of = {}
-        plane_list = []
-        for w, c0, ncols in ((0, 0, 1024), (0, 1024, 1024), (1, 0, 2048)):
-            plane = keep.tile([P, G, ncols], U8, name="plane%d_%d" % (w, c0), align_bytes=64)
-            nc.vector.memset(plane[:].rearrange("p g n -> p (g n)").bitcast(I32), 0)
-            plane_list.append((plane, w, c0, ncols))
-            for c in range(c0, c0 + ncols, NB):
-                plane_of[(w, c // NB)] = (plane, c - c0)
-
-        cos_bf = keep.tile([P, DK], BF16, name="cos_bf")
-        sin_bf = keep.tile([P, DK], BF16, name="sin_bf")
-        nc.gpsimd.dma_start(out=cos_bf[:], in_=cos2)
-        nc.gpsimd.dma_start(out=sin_bf[:], in_=sin2)
-        ident = keep.tile([P, P], F32, name="ident")
-        make_identity(nc, ident[:])
+        psum = ctx.enter_context(tc.psum_pool(name="psum", bufs=8))
+        ctx.enter_context(tc.manual_schedule())
 
         x_sb = []
         for m in range(B):
             xs = keep.tile([P, D], BF16, name="x%d" % m)
             x_sb.append(xs)
-        nc.scalar.dma_start(out=x_sb[0][:, 0:1024], in_=x[0][:, 0:1024])
-        nc.scalar.dma_start(out=x_sb[0][:, 1024:2048], in_=x[0][:, 1024:2048])
+        for piece in X0_PIECES:
+            cols = slice(512 * piece[0], 512 * (piece[-1] + 1))
+            nc.scalar.dma_start(out=x_sb[0][:, cols], in_=x[0][:, cols])
+
+        plane_of = {}
+        plane_list = []
+        for w, c0, ncols in ((0, 0, 1024), (0, 1024, 1024), (1, 0, 2048)):
+            plane = keep.tile([P, G, ncols], U8, name="plane%d_%d" % (w, c0), align_bytes=64)
+            plane_list.append((plane, w, c0, ncols))
+            for c in range(c0, c0 + ncols, NB):
+                plane_of[(w, c // NB)] = (plane, c - c0)
+
+        def fill_plane(i):
+            nc.vector.memset(plane_list[i][0][:].rearrange("p g n -> p (g n)").bitcast(I32), 0)
+
+        fill_plane(0)
+        if WARM:
+            zb = keep.tile([P, NB], BF16, name="zb")
+            nc.vector.memset(zb[:], 0.0)
+            dummy = psum.tile([P, NB], F32, name="bank")
+            for i in range(WARM):
+                nc.tensor.matmul(out=dummy[:], lhsT=zb[:, 0:P], rhs=zb[:], start=True, stop=True)
+        warm = keep.tile([P, 8], F32, name="warm")
+        warm2 = keep.tile([P, 8], F32, name="warm2")
+        nc.vector.memset(warm[:], 0.0)
+        nc.scalar.activation(out=warm2[:], in_=warm[:], func=COPY)
+        fill_plane(1)
+        fill_plane(2)
+
+        ident = keep.tile([P, P], F32, name="ident")
+        make_identity(nc, ident[:])
+        cos_bf = keep.tile([P, DK], BF16, name="cos_bf")
+        sin_bf = keep.tile([P, DK], BF16, name="sin_bf")
+        nc.gpsimd.dma_start(out=cos_bf[:], in_=cos2)
+        nc.gpsimd.dma_start(out=sin_bf[:], in_=sin2)
 
         w_sb = {}
 
         def load_scales(i):
             plane, w, c0, ncols = plane_list[i]
             for q in range(4):
-                nc.sync.dma_start(
-                    out=plane[32 * q : 32 * q + 4, :, :].bitcast(I32),
-                    in_=w_scales[w][:, 4 * q : 4 * q + 4, c0 : c0 + ncols].rearrange("g r n -> r g n").bitcast(I32),
-                )
+                if SCALES_BY_R:
+                    nc.sync.dma_start(
+                        out=plane[q : P : 32, :, :].bitcast(I32),
+                        in_=w_scales[w][:, q : 16 : 4, c0 : c0 + ncols].rearrange("g r n -> r g n").bitcast(I32),
+                    )
+                else:
+                    nc.sync.dma_start(
+                        out=plane[32 * q : 32 * q + 4, :, :].bitcast(I32),
+                        in_=w_scales[w][:, 4 * q : 4 * q + 4, c0 : c0 + ncols].rearrange("g r n -> r g n").bitcast(I32),
+                    )
 
         def load_words(w, c0, ncols):
             wt = keep.tile([P, G, 2 * ncols], U8, name="w%d_%d" % (w, c0), align_bytes=64)
@@ -131,36 +151,53 @@ def tile_multiheadselfattention_pa_kernel(
 
         x_codes = []
         x_scl = []
+        x_perm = {}
         for m in range(B):
             xc = keep.tile([P, G, P], U32, name="xc%d" % m, align_bytes=64)
             xl = keep.tile([P, G, P], U8, name="xl%d" % m, align_bytes=64)
             x_codes.append(xc)
             x_scl.append(xl)
 
-        def prep(m):
+        def permute(m):
+            xp = keep.tile([P, D // 2], F32, name="xp%d" % m)
+            for piece in XM_PIECES:
+                cols = slice(256 * piece[0], 256 * (piece[-1] + 1))
+                nc.scalar.copy(
+                    out=xp[:, cols].rearrange("p (g u q) -> p g u q", g=len(piece), u=2),
+                    in_=x_sb[m][:].bitcast(F32)[:, cols].rearrange("p (g q u) -> p g u q", g=len(piece), u=2),
+                )
+            x_perm[m] = xp
+
+        def prep(m, pieces):
             words = x_sb[m][:].bitcast(F32)
             grouped = keep.tile([P, D], BF16, name="grp%d" % m, align_bytes=64)
             gview = grouped[:].bitcast(F32).rearrange("p (g r u) -> p g r u", g=G, u=2)
-            for half in range(2):
-                xt = xt_pool.tile([P, 4, P], F32, name="xt")
-                for gg in range(2):
-                    g = 2 * half + gg
+            for piece in pieces:
+                n = len(piece)
+                g0 = piece[0]
+                xt = psum.tile([P, 4, P], F32, name="bank")
+                for gg in range(n):
+                    g = g0 + gg
                     for u in range(2):
-                        nc.tensor.transpose(xt[:, 2 * gg + u, :], words[:, 256 * g + u : 256 * (g + 1) : 2], ident[:])
+                        if m in x_perm:
+                            src = x_perm[m][:, 256 * g + 128 * u : 256 * g + 128 * (u + 1)]
+                        else:
+                            src = words[:, 256 * g + u : 256 * (g + 1) : 2]
+                        nc.tensor.transpose(xt[:, 2 * gg + u, :], src, ident[:])
                 nc.scalar.copy(
-                    out=gview[:, 2 * half : 2 * half + 2],
-                    in_=xt[:].rearrange("p (g u) r -> p g r u", u=2),
+                    out=gview[:, g0 : g0 + n],
+                    in_=xt[:, 0 : 2 * n, :].rearrange("p (g u) r -> p g r u", u=2),
                 )
                 nc.vector.quantize_mx(
-                    out=x_codes[m][:, 2 * half : 2 * half + 2, :].rearrange("p g r -> p (g r)").bitcast(E5M2X4),
-                    scales=x_scl[m][:, 2 * half : 2 * half + 2, :].rearrange("p g r -> p (g r)"),
-                    in_=grouped[:, 1024 * half : 1024 * (half + 1)],
+                    out=x_codes[m][:, g0 : g0 + n, :].rearrange("p g r -> p (g r)").bitcast(E5M2X4),
+                    scales=x_scl[m][:, g0 : g0 + n, :].rearrange("p g r -> p (g r)"),
+                    in_=grouped[:, 512 * g0 : 512 * (g0 + n)],
                 )
 
         def bank(w, m, jj, ta, tb):
             wt, off = w_sb[(w, jj)]
             plane, poff = plane_of[(w, jj)]
-            acc = acc_pool.tile([P, NB], F32, name="acc")
+            acc = psum.tile([P, NB], F32, name="bank")
             for g in range(G):
                 nc.tensor.matmul_mx(
                     out=acc[:],
@@ -180,8 +217,9 @@ def tile_multiheadselfattention_pa_kernel(
                 op=MULT,
             )
 
-        prep(0)
+        prep(0, X0_PIECES)
         sin_tables()
+        n_store = 0
         for w in range(2):
             for m in range(B):
                 ta = work.tile([P, E], F32, name="ta")
@@ -194,17 +232,29 @@ def tile_multiheadselfattention_pa_kernel(
                     adds = LAST_ADDS
                 ends = []
                 c = 0
-                for width in adds:
-                    ends.append((c, c + width))
+                for width, on_vector in adds:
+                    ends.append((c, c + width, on_vector))
                     c += width
+                late = []
                 for jj in range(NJ):
-                    if w == 0 and m + 1 < B and jj == PREP_AFTER:
-                        prep(m + 1)
+                    if w == 0 and m + 1 < B:
+                        if PERMUTE and jj == 0:
+                            permute(m + 1)
+                        if jj == PREP_AFTER:
+                            prep(m + 1, XM_PIECES)
                     bank(w, m, jj, ta, tb)
-                    for c0, c1 in ends:
-                        if c1 == NB * (jj + 1):
-                            nc.gpsimd.tensor_tensor(out=to[:, c0:c1], in0=ta[:, c0:c1], in1=tb[:, c0:c1], op=ADD)
-                            nc.sync.dma_start(
-                                out=outs[w][m, c0 // DK : c1 // DK].rearrange("h s d -> s h d"),
-                                in_=to[:, c0:c1].rearrange("p (h d) -> p h d", d=DK),
-                            )
+                    todo = [t for t in ends if t[1] == NB * (jj + 1)]
+                    if jj == NJ - 1:
+                        todo = late + todo
+                    for c0, c1, on_vector in todo:
+                        if on_vector and jj < NJ - 1:
+                            late.append((c0, c1, on_vector))
+                            continue
+                        eng = nc.vector if on_vector else nc.gpsimd
+                        eng.tensor_tensor(out=to[:, c0:c1], in0=ta[:, c0:c1], in1=tb[:, c0:c1], op=ADD)
+                        dq = nc.scalar if (STORE_ALT and n_store % 2 == 1) else nc.sync
+                        n_store += 1
+                        dq.dma_start(
+                            out=outs[w][m, c0 // DK : c1 // DK].rearrange("h s d -> s h d"),
+                            in_=to[:, c0:c1].rearrange("p (h d) -> p h d", d=DK),
+                        )

@@ -22,19 +22,14 @@ P = 128
 G = D // 512
 NB = 512
 HB = NB // DK
-NJ = E // NB
+UW = 2 * NB
 
-WORK_BUFS = 3
-PREP_AFTER = 2
-FIRST_ADDS = ((512, 0), (512, 0), (1024, 0))
-MID_ADDS = ((1024, 0), (1024, 0))
-LAST_ADDS = ((512, 0), (512, 1), (512, 1), (512, 1))
-PERMUTE = True
-WARM = 4
-X0_PIECES = ((0, 1), (2,), (3,))
-XM_PIECES = ((0, 1), (2, 3))
-SCALES_BY_R = False
-STORE_ALT = False
+WORK_BUFS = 6
+WARM1 = 4
+WARM2 = 2
+NARROW_UNITS = 2
+STORE_ON_SYNC = False
+PIECES = ((0, 1), (2, 3))
 
 
 def tile_multiheadselfattention_pa_kernel(
@@ -51,14 +46,21 @@ def tile_multiheadselfattention_pa_kernel(
         psum = ctx.enter_context(tc.psum_pool(name="psum", bufs=8))
         ctx.enter_context(tc.manual_schedule())
 
+        cos_bf = keep.tile([P, DK], BF16, name="cos_bf")
+        sin_bf = keep.tile([P, DK], BF16, name="sin_bf")
         x_sb = []
+        x_grp = []
+        x_codes = []
+        x_scl = []
         for m in range(B):
             xs = keep.tile([P, D], BF16, name="x%d" % m)
+            xg = keep.tile([P, D], BF16, name="grp%d" % m, align_bytes=64)
+            xc = keep.tile([P, G, P], U32, name="xc%d" % m, align_bytes=64)
+            xl = keep.tile([P, G, P], U8, name="xl%d" % m, align_bytes=64)
             x_sb.append(xs)
-        for piece in X0_PIECES:
-            cols = slice(512 * piece[0], 512 * (piece[-1] + 1))
-            nc.scalar.dma_start(out=x_sb[0][:, cols], in_=x[0][:, cols])
-
+            x_grp.append(xg)
+            x_codes.append(xc)
+            x_scl.append(xl)
         plane_of = {}
         plane_list = []
         for w, c0, ncols in ((0, 0, 1024), (0, 1024, 1024), (1, 0, 2048)):
@@ -66,46 +68,18 @@ def tile_multiheadselfattention_pa_kernel(
             plane_list.append((plane, w, c0, ncols))
             for c in range(c0, c0 + ncols, NB):
                 plane_of[(w, c // NB)] = (plane, c - c0)
+        w_sb = {}
 
         def fill_plane(i):
             nc.vector.memset(plane_list[i][0][:].rearrange("p g n -> p (g n)").bitcast(I32), 0)
 
-        fill_plane(0)
-        if WARM:
-            zb = keep.tile([P, NB], BF16, name="zb")
-            nc.vector.memset(zb[:], 0.0)
-            dummy = psum.tile([P, NB], F32, name="bank")
-            for i in range(WARM):
-                nc.tensor.matmul(out=dummy[:], lhsT=zb[:, 0:P], rhs=zb[:], start=True, stop=True)
-        warm = keep.tile([P, 8], F32, name="warm")
-        warm2 = keep.tile([P, 8], F32, name="warm2")
-        nc.vector.memset(warm[:], 0.0)
-        nc.scalar.activation(out=warm2[:], in_=warm[:], func=COPY)
-        fill_plane(1)
-        fill_plane(2)
-
-        ident = keep.tile([P, P], F32, name="ident")
-        make_identity(nc, ident[:])
-        cos_bf = keep.tile([P, DK], BF16, name="cos_bf")
-        sin_bf = keep.tile([P, DK], BF16, name="sin_bf")
-        nc.gpsimd.dma_start(out=cos_bf[:], in_=cos2)
-        nc.gpsimd.dma_start(out=sin_bf[:], in_=sin2)
-
-        w_sb = {}
-
         def load_scales(i):
             plane, w, c0, ncols = plane_list[i]
             for q in range(4):
-                if SCALES_BY_R:
-                    nc.sync.dma_start(
-                        out=plane[q : P : 32, :, :].bitcast(I32),
-                        in_=w_scales[w][:, q : 16 : 4, c0 : c0 + ncols].rearrange("g r n -> r g n").bitcast(I32),
-                    )
-                else:
-                    nc.sync.dma_start(
-                        out=plane[32 * q : 32 * q + 4, :, :].bitcast(I32),
-                        in_=w_scales[w][:, 4 * q : 4 * q + 4, c0 : c0 + ncols].rearrange("g r n -> r g n").bitcast(I32),
-                    )
+                nc.sync.dma_start(
+                    out=plane[32 * q : 32 * q + 4, :, :].bitcast(I32),
+                    in_=w_scales[w][:, 4 * q : 4 * q + 4, c0 : c0 + ncols].rearrange("g r n -> r g n").bitcast(I32),
+                )
 
         def load_words(w, c0, ncols):
             wt = keep.tile([P, G, 2 * ncols], U8, name="w%d_%d" % (w, c0), align_bytes=64)
@@ -116,18 +90,40 @@ def tile_multiheadselfattention_pa_kernel(
             for c in range(c0, c0 + ncols, NB):
                 w_sb[(w, c // NB)] = (wt, c - c0)
 
-        load_words(0, 0, 512)
+        def load_x(m):
+            nc.sync.dma_start(out=x_sb[m][:], in_=x[m])
+
+        def dummies(n):
+            dummy = psum.tile([P, NB], F32, name="bank")
+            for i in range(n):
+                nc.tensor.matmul(out=dummy[:], lhsT=zb[:, 0:P], rhs=zb[:], start=True, stop=True)
+
+        nc.scalar.dma_start(out=cos_bf[:], in_=cos2)
+        nc.scalar.dma_start(out=sin_bf[:], in_=sin2)
+        fill_plane(0)
+        load_x(0)
+        load_x(1)
         load_scales(0)
+        load_words(0, 0, 512)
+        load_x(2)
+        load_x(3)
         load_words(0, 512, 512)
-        nc.sync.dma_start(out=x_sb[1][:], in_=x[1])
+        zb = keep.tile([P, NB], BF16, name="zb")
+        nc.vector.memset(zb[:], 0.0)
+        dummies(WARM1)
+        warm = keep.tile([P, 8], F32, name="warm")
+        warm2 = keep.tile([P, 8], F32, name="warm2")
+        nc.vector.memset(warm[:], 0.0)
+        nc.scalar.activation(out=warm2[:], in_=warm[:], func=COPY)
+        fill_plane(1)
+        fill_plane(2)
         load_scales(1)
-        load_words(0, 1024, 512)
-        load_words(0, 1536, 512)
-        nc.sync.dma_start(out=x_sb[2][:], in_=x[2])
-        nc.sync.dma_start(out=x_sb[3][:], in_=x[3])
+        load_words(0, 1024, 1024)
         load_scales(2)
         load_words(1, 0, 1024)
         load_words(1, 1024, 1024)
+        ident = keep.tile([P, P], F32, name="ident")
+        make_identity(nc, ident[:])
 
         cos4 = keep.tile([P, HB, DK], F32, name="cos4")
         sin4 = keep.tile([P, HB, DK], F32, name="sin4")
@@ -139,51 +135,25 @@ def tile_multiheadselfattention_pa_kernel(
             op0=MULT,
             op1=ADD,
         )
+        for e, sign in ((0, -1.0), (1, 1.0)):
+            nc.scalar.activation(
+                out=sin4[:, :, e:DK:2],
+                in_=sin_bf[:, e:DK:2].rearrange("p (o d) -> p o d", o=1).to_broadcast([P, HB, DK // 2]),
+                func=COPY,
+                scale=sign,
+            )
 
-        def sin_tables():
-            for e, sign in ((0, -1.0), (1, 1.0)):
-                nc.scalar.activation(
-                    out=sin4[:, :, e:DK:2],
-                    in_=sin_bf[:, e:DK:2].rearrange("p (o d) -> p o d", o=1).to_broadcast([P, HB, DK // 2]),
-                    func=COPY,
-                    scale=sign,
-                )
-
-        x_codes = []
-        x_scl = []
-        x_perm = {}
-        for m in range(B):
-            xc = keep.tile([P, G, P], U32, name="xc%d" % m, align_bytes=64)
-            xl = keep.tile([P, G, P], U8, name="xl%d" % m, align_bytes=64)
-            x_codes.append(xc)
-            x_scl.append(xl)
-
-        def permute(m):
-            xp = keep.tile([P, D // 2], F32, name="xp%d" % m)
-            for piece in XM_PIECES:
-                cols = slice(256 * piece[0], 256 * (piece[-1] + 1))
-                nc.scalar.copy(
-                    out=xp[:, cols].rearrange("p (g u q) -> p g u q", g=len(piece), u=2),
-                    in_=x_sb[m][:].bitcast(F32)[:, cols].rearrange("p (g q u) -> p g u q", g=len(piece), u=2),
-                )
-            x_perm[m] = xp
-
-        def prep(m, pieces):
+        def prep(m):
             words = x_sb[m][:].bitcast(F32)
-            grouped = keep.tile([P, D], BF16, name="grp%d" % m, align_bytes=64)
-            gview = grouped[:].bitcast(F32).rearrange("p (g r u) -> p g r u", g=G, u=2)
-            for piece in pieces:
+            gview = x_grp[m][:].bitcast(F32).rearrange("p (g r u) -> p g r u", g=G, u=2)
+            for piece in PIECES:
                 n = len(piece)
                 g0 = piece[0]
                 xt = psum.tile([P, 4, P], F32, name="bank")
                 for gg in range(n):
                     g = g0 + gg
                     for u in range(2):
-                        if m in x_perm:
-                            src = x_perm[m][:, 256 * g + 128 * u : 256 * g + 128 * (u + 1)]
-                        else:
-                            src = words[:, 256 * g + u : 256 * (g + 1) : 2]
-                        nc.tensor.transpose(xt[:, 2 * gg + u, :], src, ident[:])
+                        nc.tensor.transpose(xt[:, 2 * gg + u, :], words[:, 256 * g + u : 256 * (g + 1) : 2], ident[:])
                 nc.scalar.copy(
                     out=gview[:, g0 : g0 + n],
                     in_=xt[:, 0 : 2 * n, :].rearrange("p (g u) r -> p g r u", u=2),
@@ -191,10 +161,19 @@ def tile_multiheadselfattention_pa_kernel(
                 nc.vector.quantize_mx(
                     out=x_codes[m][:, g0 : g0 + n, :].rearrange("p g r -> p (g r)").bitcast(E5M2X4),
                     scales=x_scl[m][:, g0 : g0 + n, :].rearrange("p g r -> p (g r)"),
-                    in_=grouped[:, 512 * g0 : 512 * (g0 + n)],
+                    in_=x_grp[m][:, 512 * g0 : 512 * (g0 + n)],
                 )
 
-        def bank(w, m, jj, ta, tb):
+        units = {}
+
+        def bank(w, m, jj):
+            key = (w, m, jj // 2)
+            if key not in units:
+                ta = work.tile([P, UW], F32, name="ta")
+                tb = work.tile([P, UW], F32, name="tb")
+                to = work.tile([P, UW], F32, name="to")
+                units[key] = (ta, tb, to)
+            ta, tb, to = units[key]
             wt, off = w_sb[(w, jj)]
             plane, poff = plane_of[(w, jj)]
             acc = psum.tile([P, NB], F32, name="bank")
@@ -208,7 +187,7 @@ def tile_multiheadselfattention_pa_kernel(
                     start=(g == 0),
                     stop=(g == G - 1),
                 )
-            cols = slice(NB * jj, NB * (jj + 1))
+            cols = slice(NB * (jj % 2), NB * (jj % 2 + 1))
             nc.vector.tensor_tensor(out=ta[:, cols], in0=acc[:], in1=cos4[:].rearrange("p h d -> p (h d)"), op=MULT)
             nc.vector.tensor_tensor(
                 out=tb[:, cols].rearrange("p (n e) -> p n e", e=2),
@@ -217,44 +196,44 @@ def tile_multiheadselfattention_pa_kernel(
                 op=MULT,
             )
 
-        prep(0, X0_PIECES)
-        sin_tables()
-        n_store = 0
-        for w in range(2):
-            for m in range(B):
-                ta = work.tile([P, E], F32, name="ta")
-                tb = work.tile([P, E], F32, name="tb")
-                to = work.tile([P, E], F32, name="to")
-                adds = MID_ADDS
-                if w == 0 and m == 0:
-                    adds = FIRST_ADDS
-                if w == 1 and m == B - 1:
-                    adds = LAST_ADDS
-                ends = []
-                c = 0
-                for width, on_vector in adds:
-                    ends.append((c, c + width, on_vector))
-                    c += width
-                late = []
-                for jj in range(NJ):
-                    if w == 0 and m + 1 < B:
-                        if PERMUTE and jj == 0:
-                            permute(m + 1)
-                        if jj == PREP_AFTER:
-                            prep(m + 1, XM_PIECES)
-                    bank(w, m, jj, ta, tb)
-                    todo = [t for t in ends if t[1] == NB * (jj + 1)]
-                    if jj == NJ - 1:
-                        todo = late + todo
-                    for c0, c1, on_vector in todo:
-                        if on_vector and jj < NJ - 1:
-                            late.append((c0, c1, on_vector))
-                            continue
-                        eng = nc.vector if on_vector else nc.gpsimd
-                        eng.tensor_tensor(out=to[:, c0:c1], in0=ta[:, c0:c1], in1=tb[:, c0:c1], op=ADD)
-                        dq = nc.scalar if (STORE_ALT and n_store % 2 == 1) else nc.sync
-                        n_store += 1
-                        dq.dma_start(
-                            out=outs[w][m, c0 // DK : c1 // DK].rearrange("h s d -> s h d"),
-                            in_=to[:, c0:c1].rearrange("p (h d) -> p h d", d=DK),
-                        )
+        def add(w, m, jp, c0, c1, eng):
+            ta, tb, to = units[(w, m, jp)]
+            eng.tensor_tensor(out=to[:, c0:c1], in0=ta[:, c0:c1], in1=tb[:, c0:c1], op=ADD)
+
+        def store(w, m, jp, c0, c1):
+            to = units[(w, m, jp)][2]
+            h0 = (UW * jp + c0) // DK
+            nc.scalar.dma_start(
+                out=outs[w][m, h0 : h0 + (c1 - c0) // DK].rearrange("h s d -> s h d"),
+                in_=to[:, c0:c1].rearrange("p (h d) -> p h d", d=DK),
+            )
+
+        def finish(w, m, jp, c0, c1, eng):
+            add(w, m, jp, c0, c1, eng)
+            store(w, m, jp, c0, c1)
+
+        prep(0)
+        prep(1)
+        if WARM2:
+            dummies(WARM2)
+        bank(0, 0, 0)
+        add(0, 0, 0, 0, NB, nc.vector)
+        prep(2)
+        prep(3)
+        store(0, 0, 0, 0, NB)
+        bank(0, 1, 0)
+        finish(0, 1, 0, 0, NB, nc.gpsimd)
+        bank(0, 0, 1)
+        finish(0, 0, 0, NB, UW, nc.gpsimd)
+        bank(0, 1, 1)
+        finish(0, 1, 0, NB, UW, nc.gpsimd)
+        rest = [(0, 0, 2), (0, 0, 3)]
+        rest += [(w, jp, m) for w, jp in ((0, 1), (1, 0), (1, 1)) for m in range(B)]
+        for i, (w, jp, m) in enumerate(rest):
+            bank(w, m, 2 * jp)
+            bank(w, m, 2 * jp + 1)
+            if i == len(rest) - 1:
+                finish(w, m, jp, 0, NB, nc.vector)
+                finish(w, m, jp, NB, UW, nc.vector)
+            else:
+                finish(w, m, jp, 0, UW, nc.gpsimd)

@@ -46,8 +46,7 @@ def tile_multiheadselfattention_pa_kernel(
         psum = ctx.enter_context(tc.psum_pool(name="psum", bufs=8))
         ctx.enter_context(tc.manual_schedule())
 
-        cos_bf = keep.tile([P, DK], BF16, name="cos_bf")
-        sin_bf = keep.tile([P, DK], BF16, name="sin_bf")
+        trig = keep.tile([P, 3 * DK + 8], BF16, name="trig")
         x_sb = []
         x_grp = []
         x_codes = []
@@ -98,8 +97,8 @@ def tile_multiheadselfattention_pa_kernel(
             for i in range(n):
                 nc.tensor.matmul(out=dummy[:], lhsT=zb[:, 0:P], rhs=zb[:], start=True, stop=True)
 
-        nc.scalar.dma_start(out=cos_bf[:], in_=cos2)
-        nc.scalar.dma_start(out=sin_bf[:], in_=sin2)
+        nc.scalar.dma_start(out=trig[:, DK : 2 * DK], in_=cos2)
+        nc.scalar.dma_start(out=trig[:, 2 * DK : 3 * DK], in_=sin2)
         fill_plane(0)
         load_x(0)
         load_x(1)
@@ -125,22 +124,20 @@ def tile_multiheadselfattention_pa_kernel(
         ident = keep.tile([P, P], F32, name="ident")
         make_identity(nc, ident[:])
 
-        cos4 = keep.tile([P, HB, DK], F32, name="cos4")
-        sin4 = keep.tile([P, HB, DK], F32, name="sin4")
+        table = keep.tile([P, 2, HB, DK], F32, name="table")
         nc.gpsimd.tensor_scalar(
-            out=cos4[:],
-            in0=cos_bf[:].rearrange("p (o d) -> p o d", o=1).to_broadcast([P, HB, DK]),
-            scalar1=1.0,
-            scalar2=0.0,
-            op0=MULT,
-            op1=ADD,
+            out=trig[:, 0:DK], in0=trig[:, 2 * DK : 3 * DK], scalar1=-1.0, scalar2=0.0, op0=MULT, op1=ADD
         )
-        for e, sign in ((0, -1.0), (1, 1.0)):
-            nc.scalar.activation(
-                out=sin4[:, :, e:DK:2],
-                in_=sin_bf[:, e:DK:2].rearrange("p (o d) -> p o d", o=1).to_broadcast([P, HB, DK // 2]),
-                func=COPY,
-                scale=sign,
+        for part in range(2):
+            base = DK * (1 - part)
+            diag = trig[:, base : base + 2 * (DK + 1)].rearrange("p (e x) -> p e x", e=2)[:, :, 0:DK:2]
+            nc.gpsimd.tensor_scalar(
+                out=table[:, part].rearrange("p h (j e) -> p h j e", e=2),
+                in0=diag.rearrange("p (o e) j -> p o j e", o=1).to_broadcast([P, HB, DK // 2, 2]),
+                scalar1=1.0,
+                scalar2=0.0,
+                op0=MULT,
+                op1=ADD,
             )
 
         def prep(m):
@@ -169,11 +166,10 @@ def tile_multiheadselfattention_pa_kernel(
         def bank(w, m, jj):
             key = (w, m, jj // 2)
             if key not in units:
-                ta = work.tile([P, UW], F32, name="ta")
-                tb = work.tile([P, UW], F32, name="tb")
+                tp = work.tile([P, UW // NB, 2, NB], F32, name="tp")
                 to = work.tile([P, UW], F32, name="to")
-                units[key] = (ta, tb, to)
-            ta, tb, to = units[key]
+                units[key] = (tp, to)
+            tp, to = units[key]
             wt, off = w_sb[(w, jj)]
             plane, poff = plane_of[(w, jj)]
             acc = psum.tile([P, NB], F32, name="bank")
@@ -187,21 +183,22 @@ def tile_multiheadselfattention_pa_kernel(
                     start=(g == 0),
                     stop=(g == G - 1),
                 )
-            cols = slice(NB * (jj % 2), NB * (jj % 2 + 1))
-            nc.vector.tensor_tensor(out=ta[:, cols], in0=acc[:], in1=cos4[:].rearrange("p h d -> p (h d)"), op=MULT)
             nc.vector.tensor_tensor(
-                out=tb[:, cols].rearrange("p (n e) -> p n e", e=2),
-                in0=acc[:].rearrange("p (n e) -> p n e", e=2)[:, :, ::-1],
-                in1=sin4[:].rearrange("p h (n e) -> p (h n) e", e=2),
+                out=tp[:, jj % 2].rearrange("p t (n e) -> p t n e", e=2),
+                in0=acc[:].rearrange("p (n t o) -> p t n o", t=2, o=1).to_broadcast([P, 2, NB // 2, 2]),
+                in1=table[:].rearrange("p t h (j e) -> p t (h j) e", e=2),
                 op=MULT,
             )
 
         def add(w, m, jp, c0, c1, eng):
-            ta, tb, to = units[(w, m, jp)]
-            eng.tensor_tensor(out=to[:, c0:c1], in0=ta[:, c0:c1], in1=tb[:, c0:c1], op=ADD)
+            tp, to = units[(w, m, jp)]
+            k0, k1 = c0 // NB, c1 // NB
+            eng.tensor_tensor(
+                out=to[:, c0:c1].rearrange("p (k n) -> p k n", n=NB), in0=tp[:, k0:k1, 0, :], in1=tp[:, k0:k1, 1, :], op=ADD
+            )
 
         def store(w, m, jp, c0, c1):
-            to = units[(w, m, jp)][2]
+            to = units[(w, m, jp)][1]
             h0 = (UW * jp + c0) // DK
             nc.scalar.dma_start(
                 out=outs[w][m, h0 : h0 + (c1 - c0) // DK].rearrange("h s d -> s h d"),

@@ -163,32 +163,47 @@ def tile_multiheadselfattention_pa_kernel(
 
         units = {}
 
-        def bank(w, m, jj):
+        def one_pass(acc, w, m, jj, g):
+            wt, off = w_sb[(w, jj)]
+            plane, poff = plane_of[(w, jj)]
+            nc.tensor.matmul_mx(
+                out=acc[:],
+                lhsT=x_codes[m][:, g, :].bitcast(E5M2X4),
+                lhsT_scale=x_scl[m][:, g, :],
+                rhs=wt[:, g, 2 * off : 2 * (off + NB)].bitcast(E2M1X4),
+                rhs_scale=plane[:, g, poff : poff + NB],
+                start=(g == 0),
+                stop=(g == G - 1),
+            )
+
+        def products(acc, w, m, jj):
             key = (w, m, jj // 2)
             if key not in units:
                 tp = work.tile([P, UW // NB, 2, NB], F32, name="tp")
                 to = work.tile([P, UW], F32, name="to")
                 units[key] = (tp, to)
             tp, to = units[key]
-            wt, off = w_sb[(w, jj)]
-            plane, poff = plane_of[(w, jj)]
-            acc = psum.tile([P, NB], F32, name="bank")
-            for g in range(G):
-                nc.tensor.matmul_mx(
-                    out=acc[:],
-                    lhsT=x_codes[m][:, g, :].bitcast(E5M2X4),
-                    lhsT_scale=x_scl[m][:, g, :],
-                    rhs=wt[:, g, 2 * off : 2 * (off + NB)].bitcast(E2M1X4),
-                    rhs_scale=plane[:, g, poff : poff + NB],
-                    start=(g == 0),
-                    stop=(g == G - 1),
-                )
             nc.vector.tensor_tensor(
                 out=tp[:, jj % 2].rearrange("p t (n e) -> p t n e", e=2),
                 in0=acc[:].rearrange("p (n t o) -> p t n o", t=2, o=1).to_broadcast([P, 2, NB // 2, 2]),
                 in1=table[:].rearrange("p t h (j e) -> p t (h j) e", e=2),
                 op=MULT,
             )
+
+        def bank(w, m, jj):
+            acc = psum.tile([P, NB], F32, name="bank")
+            for g in range(G):
+                one_pass(acc, w, m, jj, g)
+            products(acc, w, m, jj)
+
+        def two_banks(w, m, jp):
+            acc_a = psum.tile([P, NB], F32, name="bank")
+            acc_b = psum.tile([P, NB], F32, name="bank")
+            for g in range(G):
+                one_pass(acc_a, w, m, 2 * jp, g)
+                one_pass(acc_b, w, m, 2 * jp + 1, g)
+            products(acc_a, w, m, 2 * jp)
+            products(acc_b, w, m, 2 * jp + 1)
 
         def add(w, m, jp, c0, c1, eng):
             tp, to = units[(w, m, jp)]
@@ -227,10 +242,11 @@ def tile_multiheadselfattention_pa_kernel(
         rest = [(0, 0, 2), (0, 0, 3)]
         rest += [(w, jp, m) for w, jp in ((0, 1), (1, 0), (1, 1)) for m in range(B)]
         for i, (w, jp, m) in enumerate(rest):
-            bank(w, m, 2 * jp)
-            bank(w, m, 2 * jp + 1)
             if i == len(rest) - 1:
+                bank(w, m, 2 * jp)
+                bank(w, m, 2 * jp + 1)
                 finish(w, m, jp, 0, NB, nc.vector)
                 finish(w, m, jp, NB, UW, nc.vector)
             else:
+                two_banks(w, m, jp)
                 finish(w, m, jp, 0, UW, nc.gpsimd)

@@ -62,7 +62,7 @@ def tile_multiheadselfattention_pa_kernel(
             x_scl.append(xl)
         plane_of = {}
         plane_list = []
-        for w, c0, ncols in ((0, 0, 1024), (0, 1024, 1024), (1, 0, 2048)):
+        for w, c0, ncols in ((0, 0, 512), (0, 512, 512), (0, 1024, 1024), (1, 0, 2048)):
             plane = keep.tile([P, G, ncols], U8, name="plane%d_%d" % (w, c0), align_bytes=64)
             plane_list.append((plane, w, c0, ncols))
             for c in range(c0, c0 + ncols, NB):
@@ -74,10 +74,10 @@ def tile_multiheadselfattention_pa_kernel(
 
         def load_scales(i):
             plane, w, c0, ncols = plane_list[i]
-            for q in range(4):
+            for r in range(4):
                 nc.sync.dma_start(
-                    out=plane[32 * q : 32 * q + 4, :, :].bitcast(I32),
-                    in_=w_scales[w][:, 4 * q : 4 * q + 4, c0 : c0 + ncols].rearrange("g r n -> r g n").bitcast(I32),
+                    out=plane[r:P:32, :, :].bitcast(I32),
+                    in_=w_scales[w][:, r:16:4, c0 : c0 + ncols].rearrange("g q n -> q g n").bitcast(I32),
                 )
 
         def load_words(w, c0, ncols):
@@ -106,7 +106,6 @@ def tile_multiheadselfattention_pa_kernel(
         load_words(0, 0, 512)
         load_x(2)
         load_x(3)
-        load_words(0, 512, 512)
         zb = keep.tile([P, NB], BF16, name="zb")
         nc.vector.memset(zb[:], 0.0)
         dummies(WARM1)
@@ -116,9 +115,12 @@ def tile_multiheadselfattention_pa_kernel(
         nc.scalar.activation(out=warm2[:], in_=warm[:], func=COPY)
         fill_plane(1)
         fill_plane(2)
+        fill_plane(3)
         load_scales(1)
-        load_words(0, 1024, 1024)
+        load_words(0, 512, 512)
         load_scales(2)
+        load_words(0, 1024, 1024)
+        load_scales(3)
         load_words(1, 0, 1024)
         load_words(1, 1024, 1024)
         ident = keep.tile([P, P], F32, name="ident")

@@ -22,13 +22,8 @@ P = 128
 G = D // 512
 NB = 512
 HB = NB // DK
-UW = 2 * NB
 
 WORK_BUFS = 6
-WARM1 = 4
-WARM2 = 2
-NARROW_UNITS = 2
-STORE_ON_SYNC = False
 PIECES = ((0, 1), (2, 3))
 
 
@@ -108,7 +103,7 @@ def tile_multiheadselfattention_pa_kernel(
         load_x(3)
         zb = keep.tile([P, NB], BF16, name="zb")
         nc.vector.memset(zb[:], 0.0)
-        dummies(WARM1)
+        dummies(4)
         warm = keep.tile([P, 8], F32, name="warm")
         warm2 = keep.tile([P, 8], F32, name="warm2")
         nc.vector.memset(warm[:], 0.0)
@@ -163,8 +158,6 @@ def tile_multiheadselfattention_pa_kernel(
                     in_=x_grp[m][:, 512 * g0 : 512 * (g0 + n)],
                 )
 
-        units = {}
-
         def one_pass(acc, w, m, jj, g):
             wt, off = w_sb[(w, jj)]
             plane, poff = plane_of[(w, jj)]
@@ -178,77 +171,69 @@ def tile_multiheadselfattention_pa_kernel(
                 stop=(g == G - 1),
             )
 
-        def products(acc, w, m, jj):
-            key = (w, m, jj // 2)
-            if key not in units:
-                tp = work.tile([P, UW // NB, 2, NB], F32, name="tp")
-                to = work.tile([P, UW], F32, name="to")
-                units[key] = (tp, to)
-            tp, to = units[key]
+        def products(acc, tp, slot):
             nc.vector.tensor_tensor(
-                out=tp[:, jj % 2].rearrange("p t (n e) -> p t n e", e=2),
+                out=tp[:, slot].rearrange("p t (n e) -> p t n e", e=2),
                 in0=acc[:].rearrange("p (n t o) -> p t n o", t=2, o=1).to_broadcast([P, 2, NB // 2, 2]),
                 in1=table[:].rearrange("p t h (j e) -> p t (h j) e", e=2),
                 op=MULT,
             )
 
-        def bank(w, m, jj):
-            acc = psum.tile([P, NB], F32, name="bank")
-            for g in range(G):
-                one_pass(acc, w, m, jj, g)
-            products(acc, w, m, jj)
+        def open_group(banks, paired):
+            n = len(banks)
+            tp = work.tile([P, n, 2, NB], F32, name="tp")
+            to = work.tile([P, n, NB], F32, name="to")
+            step = 2 if paired else 1
+            for i in range(0, n, step):
+                accs = []
+                for k in range(step):
+                    acc = psum.tile([P, NB], F32, name="bank")
+                    accs.append(acc)
+                for g in range(G):
+                    for k in range(step):
+                        w, m, jj = banks[i + k]
+                        one_pass(accs[k], w, m, jj, g)
+                for k in range(step):
+                    products(accs[k], tp, i + k)
+            return (banks, tp, to)
 
-        def two_banks(w, m, jp):
-            acc_a = psum.tile([P, NB], F32, name="bank")
-            acc_b = psum.tile([P, NB], F32, name="bank")
-            for g in range(G):
-                one_pass(acc_a, w, m, 2 * jp, g)
-                one_pass(acc_b, w, m, 2 * jp + 1, g)
-            products(acc_a, w, m, 2 * jp)
-            products(acc_b, w, m, 2 * jp + 1)
+        def add(grp, lo, hi, eng):
+            banks, tp, to = grp
+            eng.tensor_tensor(out=to[:, lo:hi, :], in0=tp[:, lo:hi, 0, :], in1=tp[:, lo:hi, 1, :], op=ADD)
 
-        def add(w, m, jp, c0, c1, eng):
-            tp, to = units[(w, m, jp)]
-            k0, k1 = c0 // NB, c1 // NB
-            eng.tensor_tensor(
-                out=to[:, c0:c1].rearrange("p (k n) -> p k n", n=NB), in0=tp[:, k0:k1, 0, :], in1=tp[:, k0:k1, 1, :], op=ADD
+        def store(grp, lo, hi, queue):
+            banks, tp, to = grp
+            w, m, jj = banks[lo]
+            queue.dma_start(
+                out=outs[w][m, HB * jj : HB * (jj + hi - lo)].rearrange("h s d -> s h d"),
+                in_=to[:, lo:hi, :].rearrange("p k (h d) -> p (k h) d", d=DK),
             )
-
-        def store(w, m, jp, c0, c1):
-            to = units[(w, m, jp)][1]
-            h0 = (UW * jp + c0) // DK
-            nc.scalar.dma_start(
-                out=outs[w][m, h0 : h0 + (c1 - c0) // DK].rearrange("h s d -> s h d"),
-                in_=to[:, c0:c1].rearrange("p (h d) -> p h d", d=DK),
-            )
-
-        def finish(w, m, jp, c0, c1, eng):
-            add(w, m, jp, c0, c1, eng)
-            store(w, m, jp, c0, c1)
 
         prep(0)
         prep(1)
-        if WARM2:
-            dummies(WARM2)
-        bank(0, 0, 0)
-        add(0, 0, 0, 0, NB, nc.vector)
+        dummies(2)
+        first = open_group([(0, 0, 0)], False)
+        add(first, 0, 1, nc.vector)
         prep(2)
         prep(3)
-        store(0, 0, 0, 0, NB)
-        bank(0, 1, 0)
-        finish(0, 1, 0, 0, NB, nc.gpsimd)
-        bank(0, 0, 1)
-        finish(0, 0, 0, NB, UW, nc.gpsimd)
-        bank(0, 1, 1)
-        finish(0, 1, 0, NB, UW, nc.gpsimd)
-        rest = [(0, 0, 2), (0, 0, 3)]
-        rest += [(w, jp, m) for w, jp in ((0, 1), (1, 0), (1, 1)) for m in range(B)]
-        for i, (w, jp, m) in enumerate(rest):
-            if i == len(rest) - 1:
-                bank(w, m, 2 * jp)
-                bank(w, m, 2 * jp + 1)
-                finish(w, m, jp, 0, NB, nc.vector)
-                finish(w, m, jp, NB, UW, nc.vector)
-            else:
-                two_banks(w, m, jp)
-                finish(w, m, jp, 0, UW, nc.gpsimd)
+        store(first, 0, 1, nc.scalar)
+        for bank in ((0, 1, 0), (0, 0, 1), (0, 1, 1)):
+            grp = open_group([bank], False)
+            add(grp, 0, 1, nc.gpsimd)
+            store(grp, 0, 1, nc.scalar)
+        units = [[(w, m, 2 * jp), (w, m, 2 * jp + 1)] for w in range(2) for jp in range(2) for m in range(B)][2:]
+        late = []
+        for pair in units[:-2]:
+            grp = open_group(pair, True)
+            add(grp, 0, 2, nc.gpsimd)
+            store(grp, 0, 2, nc.scalar)
+        grp = open_group(units[-2], True)
+        add(grp, 0, 1, nc.gpsimd)
+        store(grp, 0, 1, nc.scalar)
+        late.append((grp, 1))
+        grp = open_group(units[-1], False)
+        late.append((grp, 0))
+        late.append((grp, 1))
+        for grp, k in late:
+            add(grp, k, k + 1, nc.vector)
+            store(grp, k, k + 1, nc.sync)

@@ -224,10 +224,10 @@ def tile_multiheadselfattention_pa_kernel(
         units = [[(w, m, 2 * jp), (w, m, 2 * jp + 1)] for w in range(2) for jp in range(2) for m in range(B)][2:]
         late = []
         for pair in units[:-2]:
-            grp = open_group(pair, True)
+            grp = open_group(pair, False)
             add(grp, 0, 2, nc.gpsimd)
             store(grp, 0, 2, nc.scalar)
-        grp = open_group(units[-2], True)
+        grp = open_group(units[-2], False)
         add(grp, 0, 1, nc.gpsimd)
         store(grp, 0, 1, nc.scalar)
         late.append((grp, 1))

@@ -84,6 +84,16 @@ def tile_multiheadselfattention_pa_kernel(
             for c in range(c0, c0 + ncols, NB):
                 w_sb[(w, c // NB)] = (wt, c - c0)
 
+        def load_all_words(w):
+            wt = keep.tile([P, G, 2 * E], U8, name="w%d" % w, align_bytes=64)
+            for g in range(0, G, 2):
+                nc.sync.dma_start(
+                    out=wt[:, g : g + 2, :].bitcast(I32),
+                    in_=w_words[w][g : g + 2].rearrange("g p n -> p g n").bitcast(I32),
+                )
+            for c in range(0, E, NB):
+                w_sb[(w, c // NB)] = (wt, c)
+
         def load_x(m):
             nc.sync.dma_start(out=x_sb[m][:], in_=x[m])
 
@@ -116,8 +126,7 @@ def tile_multiheadselfattention_pa_kernel(
         load_scales(2)
         load_words(0, 1024, 1024)
         load_scales(3)
-        load_words(1, 0, 1024)
-        load_words(1, 1024, 1024)
+        load_all_words(1)
         ident = keep.tile([P, P], F32, name="ident")
         make_identity(nc, ident[:])
 
@@ -223,10 +232,10 @@ def tile_multiheadselfattention_pa_kernel(
             store(grp, 0, 1, nc.scalar)
         units = [[(w, m, 2 * jp), (w, m, 2 * jp + 1)] for w in range(2) for jp in range(2) for m in range(B)][2:]
         late = []
-        for pair in units[:-2]:
+        for i, pair in enumerate(units[:-2]):
             grp = open_group(pair, False)
             add(grp, 0, 2, nc.gpsimd)
-            store(grp, 0, 2, nc.scalar)
+            store(grp, 0, 2, (nc.scalar, nc.sync)[i % 2])
         grp = open_group(units[-2], False)
         add(grp, 0, 1, nc.gpsimd)
         store(grp, 0, 1, nc.scalar)

from contextlib import ExitStack

import concourse.mybir as mybir
from concourse.masks import make_identity

B, S, D, H, DK = 4, 128, 2048, 16, 128
E = H * DK
FLOPS = 2 * (B * S) * D * (2 * E)

F32 = mybir.dt.float32
BF16 = mybir.dt.bfloat16
U32 = mybir.dt.uint32
U8 = mybir.dt.uint8
I32 = mybir.dt.int32
E5M2X4 = mybir.dt.float8_e5m2_x4
E2M1X4 = mybir.dt.float4_e2m1fn_x4
MULT = mybir.AluOpType.mult
ADD = mybir.AluOpType.add
COPY = mybir.ActivationFunctionType.Copy

P = 128
G = D // 512
NB = 512
HB = NB // DK

WORK_BUFS = 6
PIECES = ((0, 1), (2, 3))


def tile_multiheadselfattention_pa_kernel(
    tc, x, Wq_words, Wq_scales, Wk_words, Wk_scales, cos2, sin2, out_0, out_1
):
    nc = tc.nc
    w_words = (Wq_words, Wk_words)
    w_scales = (Wq_scales, Wk_scales)
    outs = (out_0, out_1)

    with ExitStack() as ctx:
        keep = ctx.enter_context(tc.tile_pool(name="keep", bufs=1))
        work = ctx.enter_context(tc.tile_pool(name="work", bufs=WORK_BUFS))
        psum = ctx.enter_context(tc.psum_pool(name="psum", bufs=8))
        ctx.enter_context(tc.manual_schedule())

        trig = keep.tile([P, 3 * DK + 8], BF16, name="trig")
        x_sb = []
        x_grp = []
        x_codes = []
        x_scl = []
        for m in range(B):
            xs = keep.tile([P, D], BF16, name="x%d" % m)
            xg = keep.tile([P, D], BF16, name="grp%d" % m, align_bytes=64)
            xc = keep.tile([P, G, P], U32, name="xc%d" % m, align_bytes=64)
            xl = keep.tile([P, G, P], U8, name="xl%d" % m, align_bytes=64)
            x_sb.append(xs)
            x_grp.append(xg)
            x_codes.append(xc)
            x_scl.append(xl)
        plane_of = {}
        plane_list = []
        for w, c0, ncols in ((0, 0, 512), (0, 512, 512), (0, 1024, 1024), (1, 0, 2048)):
            plane = keep.tile([P, G, ncols], U8, name="plane%d_%d" % (w, c0), align_bytes=64)
            plane_list.append((plane, w, c0, ncols))
            for c in range(c0, c0 + ncols, NB):
                plane_of[(w, c // NB)] = (plane, c - c0)
        w_sb = {}

        def fill_plane(i):
            nc.vector.memset(plane_list[i][0][:].rearrange("p g n -> p (g n)").bitcast(I32), 0)

        def load_scales(i):
            plane, w, c0, ncols = plane_list[i]
            for r in range(4):
                nc.sync.dma_start(
                    out=plane[r:P:32, :, :].bitcast(I32),
                    in_=w_scales[w][:, r:16:4, c0 : c0 + ncols].rearrange("g q n -> q g n").bitcast(I32),
                )

        def load_words(w, c0, ncols):
            wt = keep.tile([P, G, 2 * ncols], U8, name="w%d_%d" % (w, c0), align_bytes=64)
            nc.sync.dma_start(
                out=wt[:].bitcast(I32),
                in_=w_words[w][:, :, 2 * c0 : 2 * (c0 + ncols)].rearrange("g p n -> p g n").bitcast(I32),
            )
            for c in range(c0, c0 + ncols, NB):
                w_sb[(w, c // NB)] = (wt, c - c0)

        def load_all_words(w):
            wt = keep.tile([P, G, 2 * E], U8, name="w%d" % w, align_bytes=64)
            for g in range(0, G, 2):
                nc.sync.dma_start(
                    out=wt[:, g : g + 2, :].bitcast(I32),
                    in_=w_words[w][g : g + 2].rearrange("g p n -> p g n").bitcast(I32),
                )
            for c in range(0, E, NB):
                w_sb[(w, c // NB)] = (wt, c)

        def load_x(m):
            nc.sync.dma_start(out=x_sb[m][:], in_=x[m])

        def dummies(n):
            dummy = psum.tile([P, NB], F32, name="bank")
            for i in range(n):
                nc.tensor.matmul(out=dummy[:], lhsT=zb[:, 0:P], rhs=zb[:], start=True, stop=True)

        nc.scalar.dma_start(out=trig[:, DK : 2 * DK], in_=cos2)
        nc.scalar.dma_start(out=trig[:, 2 * DK : 3 * DK], in_=sin2)
        fill_plane(0)
        load_x(0)
        load_x(1)
        load_scales(0)
        load_words(0, 0, 512)
        load_x(2)
        load_x(3)
        zb = keep.tile([P, NB], BF16, name="zb")
        nc.vector.memset(zb[:], 0.0)
        dummies(4)
        warm = keep.tile([P, 8], F32, name="warm")
        warm2 = keep.tile([P, 8], F32, name="warm2")
        nc.vector.memset(warm[:], 0.0)
        nc.scalar.activation(out=warm2[:], in_=warm[:], func=COPY)
        fill_plane(1)
        fill_plane(2)
        fill_plane(3)
        load_scales(1)
        load_words(0, 512, 512)
        load_scales(2)
        load_words(0, 1024, 1024)
        load_scales(3)
        load_all_words(1)
        ident = keep.tile([P, P], F32, name="ident")
        make_identity(nc, ident[:])

        table = keep.tile([P, 2, HB, DK], F32, name="table")
        nc.gpsimd.tensor_scalar(
            out=trig[:, 0:DK], in0=trig[:, 2 * DK : 3 * DK], scalar1=-1.0, scalar2=0.0, op0=MULT, op1=ADD
        )
        for part in range(2):
            base = DK * (1 - part)
            diag = trig[:, base : base + 2 * (DK + 1)].rearrange("p (e x) -> p e x", e=2)[:, :, 0:DK:2]
            nc.gpsimd.tensor_scalar(
                out=table[:, part].rearrange("p h (j e) -> p h j e", e=2),
                in0=diag.rearrange("p (o e) j -> p o j e", o=1).to_broadcast([P, HB, DK // 2, 2]),
                scalar1=1.0,
                scalar2=0.0,
                op0=MULT,
                op1=ADD,
            )

        def prep(m):
            words = x_sb[m][:].bitcast(F32)
            gview = x_grp[m][:].bitcast(F32).rearrange("p (g r u) -> p g r u", g=G, u=2)
            for piece in PIECES:
                n = len(piece)
                g0 = piece[0]
                xt = psum.tile([P, 4, P], F32, name="bank")
                for gg in range(n):
                    g = g0 + gg
                    for u in range(2):
                        nc.tensor.transpose(xt[:, 2 * gg + u, :], words[:, 256 * g + u : 256 * (g + 1) : 2], ident[:])
                nc.scalar.copy(
                    out=gview[:, g0 : g0 + n],
                    in_=xt[:, 0 : 2 * n, :].rearrange("p (g u) r -> p g r u", u=2),
                )
                nc.vector.quantize_mx(
                    out=x_codes[m][:, g0 : g0 + n, :].rearrange("p g r -> p (g r)").bitcast(E5M2X4),
                    scales=x_scl[m][:, g0 : g0 + n, :].rearrange("p g r -> p (g r)"),
                    in_=x_grp[m][:, 512 * g0 : 512 * (g0 + n)],
                )

        def one_pass(acc, w, m, jj, g):
            wt, off = w_sb[(w, jj)]
            plane, poff = plane_of[(w, jj)]
            nc.tensor.matmul_mx(
                out=acc[:],
                lhsT=x_codes[m][:, g, :].bitcast(E5M2X4),
                lhsT_scale=x_scl[m][:, g, :],
                rhs=wt[:, g, 2 * off : 2 * (off + NB)].bitcast(E2M1X4),
                rhs_scale=plane[:, g, poff : poff + NB],
                start=(g == 0),
                stop=(g == G - 1),
            )

        def products(acc, tp, slot):
            nc.vector.tensor_tensor(
                out=tp[:, slot].rearrange("p t (n e) -> p t n e", e=2),
                in0=acc[:].rearrange("p (n t o) -> p t n o", t=2, o=1).to_broadcast([P, 2, NB // 2, 2]),
                in1=table[:].rearrange("p t h (j e) -> p t (h j) e", e=2),
                op=MULT,
            )

        def open_group(banks, paired):
            n = len(banks)
            tp = work.tile([P, n, 2, NB], F32, name="tp")
            to = work.tile([P, n, NB], F32, name="to")
            step = 2 if paired else 1
            for i in range(0, n, step):
                accs = []
                for k in range(step):
                    acc = psum.tile([P, NB], F32, name="bank")
                    accs.append(acc)
                for g in range(G):
                    for k in range(step):
                        w, m, jj = banks[i + k]
                        one_pass(accs[k], w, m, jj, g)
                for k in range(step):
                    products(accs[k], tp, i + k)
            return (banks, tp, to)

        def add(grp, lo, hi, eng):
            banks, tp, to = grp
            eng.tensor_tensor(out=to[:, lo:hi, :], in0=tp[:, lo:hi, 0, :], in1=tp[:, lo:hi, 1, :], op=ADD)

        def store(grp, lo, hi, queue):
            banks, tp, to = grp
            w, m, jj = banks[lo]
            queue.dma_start(
                out=outs[w][m, HB * jj : HB * (jj + hi - lo)].rearrange("h s d -> s h d"),
                in_=to[:, lo:hi, :].rearrange("p k (h d) -> p (k h) d", d=DK),
            )

        prep(0)
        prep(1)
        dummies(2)
        first = open_group([(0, 0, 0)], False)
        add(first, 0, 1, nc.vector)
        prep(2)
        prep(3)
        store(first, 0, 1, nc.scalar)
        for bank in ((0, 1, 0), (0, 0, 1), (0, 1, 1)):
            grp = open_group([bank], False)
            add(grp, 0, 1, nc.gpsimd)
            store(grp, 0, 1, nc.scalar)
        units = [[(w, m, 2 * jp), (w, m, 2 * jp + 1)] for w in range(2) for jp in range(2) for m in range(B)][2:]
        late = []
        for i, pair in enumerate(units[:-2]):
            grp = open_group(pair, False)
            add(grp, 0, 2, nc.gpsimd)
            store(grp, 0, 2, (nc.scalar, nc.sync)[i % 2])
        grp = open_group(units[-2], False)
        add(grp, 0, 1, nc.gpsimd)
        store(grp, 0, 1, nc.scalar)
        late.append((grp, 1))
        grp = open_group(units[-1], False)
        late.append((grp, 0))
        late.append((grp, 1))
        for grp, k in late:
            add(grp, k, k + 1, nc.vector)
            store(grp, k, k + 1, nc.sync)
